import numpy as np
import ml_dtypes


def mxq(x, axis, fmt="e4m3"):
    dtype, down = {"e4m3": (ml_dtypes.float8_e4m3fn, 7), "e5m2": (ml_dtypes.float8_e5m2, 14)}[fmt]
    v = np.moveaxis(np.asarray(x, np.float32).astype(ml_dtypes.bfloat16).astype(np.float64), axis, -1)
    blocks = v.reshape(v.shape[:-1] + (-1, 32))
    amax = np.abs(blocks).max(-1, keepdims=True)
    byte = np.maximum(np.where(amax > 0, np.frexp(amax)[1] - 1 + 127, 0) - down, 1)
    scale = np.exp2(byte - 127.0)
    codes = (blocks / scale).astype(np.float32).astype(dtype).astype(np.float64)
    return np.moveaxis((codes * scale).reshape(v.shape), -1, axis)


WIDE = False


def mx_kscale(k):
    if not WIDE:
        return np.ones(k)
    levels = np.array([10, -10, 5, -5, 0])
    a = np.random.permutation(np.resize(levels, k // 512 * 4)).reshape(k // 512, 4)
    idx = np.arange(k)
    return np.exp2(a[idx // 512, idx % 128 // 32])


BF16 = ml_dtypes.bfloat16


def bf(x):
    return np.asarray(x, np.float32).astype(BF16)


def f64(x):
    return np.asarray(x).astype(np.float64)


B, N, HD, NH, KVH, D = 8, 512, 512, 8, 2, 128
QD = NH * D
KVD = KVH * D
EPS = 2.0 ** -23


def setup_inputs():
    s = mx_kscale(HD)
    rows = np.exp2(np.random.uniform(-2.0, 2.0, (B, N, 1)))
    rows = np.where(np.random.random((B, N, 1)) < 0.125, rows * 2.0 ** -11, rows)
    return {"tokens": bf(np.random.standard_normal((B, N, HD)) * rows),
            "norm_w": bf((1.0 + 0.1 * np.random.standard_normal(HD)) * s),
            "Wq": bf(np.random.standard_normal((QD, HD)) * 0.4 / np.sqrt(HD) / s[None, :]),
            "bq": bf(np.random.standard_normal(QD) * 0.1),
            "Wk": bf(np.random.standard_normal((KVD, HD)) * 0.4 / np.sqrt(HD) / s[None, :]),
            "bk": bf(np.random.standard_normal(KVD) * 0.1),
            "Wv": bf(np.random.standard_normal((KVD, HD)) / np.sqrt(HD) / s[None, :]),
            "bv": bf(np.random.standard_normal(KVD) * 0.3)}


def reference(tokens, norm_w, Wq, bq, Wk, bk, Wv, bv):
    t = f64(tokens)
    x = t / np.sqrt(np.mean(t * t, axis=-1, keepdims=True) + EPS) * f64(norm_w)
    xq = mxq(x, 2, "e4m3")
    q = ((xq @ mxq(f64(Wq), 1, "e4m3").T) + f64(bq)).reshape(B, N, NH, D).transpose(0, 2, 1, 3)
    k = ((xq @ mxq(f64(Wk), 1, "e4m3").T) + f64(bk)).reshape(B, N, KVH, D).transpose(0, 2, 1, 3)
    v = ((xq @ mxq(f64(Wv), 1, "e4m3").T) + f64(bv)).reshape(B, N, KVH, D).transpose(0, 2, 1, 3)
    return q, k, v

@@ -1,0 +1,268 @@
+from contextlib import ExitStack
+
+import concourse.masks as masks
+import concourse.mybir as mybir
+
+F32 = mybir.dt.float32
+BF16 = mybir.dt.bfloat16
+U32 = mybir.dt.uint32
+U8 = mybir.dt.uint8
+FP8X4 = mybir.dt.float8_e4m3fn_x4
+ACT = mybir.ActivationFunctionType
+ALU = mybir.AluOpType
+
+P = 128
+BATCHES = 8
+TOKENS = 512
+HIDDEN = 512
+HEAD = 128
+Q_HEADS = 8
+KV_HEADS = 2
+EPS = 2.0**-23
+
+TILES = TOKENS // P
+PACK = 4
+HALVES = 2
+GROUP_HEADS = 4
+GROUP = GROUP_HEADS * HEAD
+COLUMNS = (Q_HEADS + 2 * KV_HEADS) * HEAD
+GROUPS = COLUMNS // GROUP
+Q_GROUPS = Q_HEADS // GROUP_HEADS
+QUANT = TILES * P * PACK
+
+FLOPS = 2 * BATCHES * TOKENS * HIDDEN * COLUMNS
+
+
+def tile_attentionlayerdecoder_pa_t_kernel(
+    tc, tokens, norm_w, Wq, bq, Wk, bk, Wv, bv, q_out, k_out, v_out
+):
+    nc = tc.nc
+    with ExitStack() as ctx:
+        ctx.enter_context(tc.manual_schedule())
+        const = ctx.enter_context(tc.tile_pool(name="const", bufs=1))
+        stats = ctx.enter_context(tc.tile_pool(name="stats", bufs=3))
+        squares = ctx.enter_context(tc.tile_pool(name="squares", bufs=4))
+        gained = ctx.enter_context(tc.tile_pool(name="gained", bufs=3))
+        normed = ctx.enter_context(tc.tile_pool(name="normed", bufs=2))
+        packed = ctx.enter_context(tc.tile_pool(name="packed", bufs=2))
+        results = ctx.enter_context(tc.tile_pool(name="results", bufs=6))
+        flipped = ctx.enter_context(tc.psum_pool(name="flipped", bufs=3))
+        sums = ctx.enter_context(tc.psum_pool(name="sums", bufs=5))
+
+        eps = const.tile([P, 1], F32)
+        nc.vector.memset(eps[:], EPS)
+        gain_row = const.tile([P, HIDDEN], BF16)
+        nc.vector.memset(gain_row[:], 0.0)
+        bias_row = const.tile([P, COLUMNS], BF16)
+        nc.vector.memset(bias_row[:], 0.0)
+        ones = const.tile([P, P], BF16)
+        nc.vector.memset(ones[:], 1.0)
+        ident = const.tile([P, P], F32)
+        masks.make_identity(nc, ident[:])
+
+        nc.scalar.dma_start(out=gain_row[0:1, :], in_=norm_w.unsqueeze(0))
+        q_columns = Q_HEADS * HEAD
+        kv_columns = KV_HEADS * HEAD
+        nc.scalar.dma_start(out=bias_row[0:1, 0:q_columns], in_=bq.unsqueeze(0))
+        nc.scalar.dma_start(
+            out=bias_row[0:1, q_columns : q_columns + kv_columns], in_=bk.unsqueeze(0)
+        )
+        nc.scalar.dma_start(out=bias_row[0:1, q_columns + kv_columns : COLUMNS], in_=bv.unsqueeze(0))
+
+        table_warm = const.tile([P, 1], F32)
+        nc.scalar.activation(out=table_warm[:], in_=eps[:], func=ACT.Sqrt)
+
+        token_tiles = {}
+
+        def load_tokens(b):
+            token_tiles[b] = const.tile([P, TILES, HIDDEN], BF16, name="tokens%d" % b)
+            nc.sync.dma_start(
+                out=token_tiles[b][:], in_=tokens[b].rearrange("(p j) k -> p j k", j=TILES)
+            )
+
+        w_raw = const.tile([P, COLUMNS // P * HIDDEN], BF16)
+        w_rows = w_raw[:].rearrange("p (r k) -> p r k", k=HIDDEN)
+
+        def load_weight_rows(first_tile, rows):
+            n_tiles = rows.shape[0] // P
+            nc.sync.dma_start(
+                out=w_rows[:, first_tile : first_tile + n_tiles, :],
+                in_=rows.rearrange("(r p) k -> p r k", p=P),
+            )
+
+        load_tokens(0)
+        load_tokens(1)
+        for g in range(Q_GROUPS):
+            load_weight_rows(g * GROUP_HEADS, Wq[g * GROUP : (g + 1) * GROUP, :])
+        load_weight_rows(Q_HEADS, Wk)
+        load_weight_rows(Q_HEADS + KV_HEADS, Wv)
+        for b in range(2, BATCHES):
+            load_tokens(b)
+
+        def repeat_row(row, out):
+            spread = sums.tile([P, GROUP], F32, name="acc")
+            nc.tensor.matmul(out=spread[:], lhsT=ones[:], rhs=row, start=True, stop=True)
+            nc.vector.tensor_copy(out=out, in_=spread[:])
+
+        gain = const.tile([P, HIDDEN], BF16)
+        repeat_row(gain_row[:], gain[:])
+        bias = const.tile([P, COLUMNS], F32)
+        for g in range(GROUPS):
+            repeat_row(bias_row[:, g * GROUP : (g + 1) * GROUP], bias[:, g * GROUP : (g + 1) * GROUP])
+
+        square_sum, root, inverse_root, gained_tokens = {}, {}, {}, {}
+        x_codes, x_scales = {}, {}
+
+        def apply_gain(b):
+            gained_tokens[b] = gained.tile([P, TILES, HIDDEN], F32, name="gained_tokens")
+            for j in range(TILES):
+                nc.gpsimd.tensor_tensor(
+                    out=gained_tokens[b][:, j, :], in0=token_tiles[b][:, j, :], in1=gain[:], op=ALU.mult
+                )
+
+        def sum_squares(b, tiles):
+            if b not in square_sum:
+                square_sum[b] = stats.tile([P, TILES], F32, name="square_sum")
+            for j in tiles:
+                unread = squares.tile([P, HIDDEN], BF16, name="unread")
+                nc.scalar.activation(
+                    out=unread[:],
+                    in_=token_tiles[b][:, j, :],
+                    func=ACT.Square,
+                    accum_out=square_sum[b][:, j : j + 1],
+                )
+
+        def root_mean_square(b):
+            root[b] = stats.tile([P, TILES], F32, name="root")
+            nc.scalar.activation(
+                out=root[b][:], in_=square_sum[b][:], func=ACT.Sqrt, bias=eps[:], scale=1.0 / HIDDEN
+            )
+
+        def invert_root(b):
+            inverse_root[b] = stats.tile([P, TILES], F32, name="inverse_root")
+            nc.vector.reciprocal(out=inverse_root[b][:], in_=root[b][:])
+
+        def k_to_partitions(row_words, grouped_words, copy):
+            for pair in range(TILES // 2):
+                flip = flipped.tile([P, 2, HALVES, P], F32, name="flip")
+                for i in range(2):
+                    for u in range(HALVES):
+                        nc.tensor.transpose(
+                            out=flip[:, i, u, :],
+                            in_=row_words[:, 2 * pair + i, u * P : (u + 1) * P],
+                            identity=ident[:],
+                        )
+                copy(
+                    out=grouped_words[:, 2 * pair : 2 * pair + 2, :, :],
+                    in_=flip[:].rearrange("p i u n -> p i n u"),
+                )
+
+        def as_row_words(tile_2d):
+            return tile_2d.bitcast(F32).rearrange("p (i w) -> p i w", i=TILES)
+
+        def as_grouped_words(tile_2d):
+            return tile_2d.bitcast(F32).rearrange("p (i n u) -> p i n u", i=TILES, u=HALVES)
+
+        def normalise(b):
+            x = normed.tile([P, TILES * HIDDEN], BF16, name="x")
+            for j in range(TILES):
+                nc.scalar.activation(
+                    out=x[:, j * HIDDEN : (j + 1) * HIDDEN],
+                    in_=gained_tokens[b][:, j, :],
+                    func=ACT.Copy,
+                    scale=inverse_root[b][:, j : j + 1],
+                )
+            return x
+
+        def pack_x(b, x):
+            grouped = normed.tile([P, QUANT], BF16, name="grouped", align_bytes=64)
+            k_to_partitions(as_row_words(x[:]), as_grouped_words(grouped[:]), nc.scalar.copy)
+            x_codes[b] = packed.tile([P, TILES * P], U32, name="x_codes", align_bytes=64)
+            x_scales[b] = packed.tile([P, TILES * P], U8, name="x_scales", align_bytes=64)
+            nc.vector.quantize_mx(
+                out=x_codes[b][:].bitcast(FP8X4), scales=x_scales[b][:], in_=grouped[:]
+            )
+
+        w_grouped = const.tile([P, GROUPS * QUANT], BF16, align_bytes=64)
+        w_codes = const.tile([P, COLUMNS], U32, align_bytes=64)
+        w_scales = const.tile([P, COLUMNS], U8, align_bytes=64)
+
+        def pack_weights(g):
+            k_to_partitions(
+                as_row_words(w_raw[:, g * GROUP_HEADS * HIDDEN : (g + 1) * GROUP_HEADS * HIDDEN]),
+                as_grouped_words(w_grouped[:, g * QUANT : (g + 1) * QUANT]),
+                nc.vector.tensor_copy,
+            )
+            nc.vector.quantize_mx(
+                out=w_codes[:, g * GROUP : (g + 1) * GROUP].bitcast(FP8X4),
+                scales=w_scales[:, g * GROUP : (g + 1) * GROUP],
+                in_=w_grouped[:, g * QUANT : (g + 1) * QUANT],
+            )
+
+        def by_head(columns):
+            return columns.rearrange("p (h d) -> p h d", d=HEAD)
+
+        def store(heads_out, y_heads):
+            nc.sync.dma_start(
+                out=heads_out.rearrange("h (p j) d -> p h (j d)", j=TILES),
+                in_=y_heads.rearrange("p h j d -> p h (j d)"),
+            )
+
+        def project(b, g):
+            columns = slice(g * GROUP, (g + 1) * GROUP)
+            y = results.tile([P, GROUP_HEADS, TILES, HEAD], F32, name="y")
+            for j in range(TILES):
+                rows = slice(j * P, (j + 1) * P)
+                acc = sums.tile([P, GROUP], F32, name="acc")
+                nc.tensor.matmul_mx(
+                    out=acc[:],
+                    lhsT=x_codes[b][:, rows].bitcast(FP8X4),
+                    lhsT_scale=x_scales[b][:, rows],
+                    rhs=w_codes[:, columns].bitcast(FP8X4),
+                    rhs_scale=w_scales[:, columns],
+                    start=True,
+                    stop=True,
+                )
+                nc.vector.tensor_tensor(
+                    out=y[:, :, j, :], in0=by_head(acc[:]), in1=by_head(bias[:, columns]), op=ALU.add
+                )
+            if g < Q_GROUPS:
+                store(q_out[b, g * GROUP_HEADS : (g + 1) * GROUP_HEADS], y[:])
+            else:
+                store(k_out[b], y[:, 0:KV_HEADS])
+                store(v_out[b], y[:, KV_HEADS : 2 * KV_HEADS])
+
+        first_half = range(0, TILES // 2)
+        second_half = range(TILES // 2, TILES)
+
+        def finish_stats(b):
+            if b < BATCHES:
+                sum_squares(b, second_half)
+                root_mean_square(b)
+            if b + 1 < BATCHES:
+                sum_squares(b + 1, first_half)
+
+        gain_ahead = 3
+        for b in range(gain_ahead):
+            apply_gain(b)
+        sum_squares(0, first_half)
+        finish_stats(0)
+        invert_root(0)
+        for g in range(GROUPS):
+            pack_weights(g)
+        pack_x(0, normalise(0))
+        finish_stats(1)
+
+        for b in range(BATCHES):
+            following = b + 1 < BATCHES
+            if following:
+                invert_root(b + 1)
+                x_next = normalise(b + 1)
+            project(b, 0)
+            project(b, 1)
+            if following:
+                pack_x(b + 1, x_next)
+            finish_stats(b + 2)
+            project(b, 2)
+            if b + gain_ahead < BATCHES:
+                apply_gain(b + gain_ahead)

@@ -29,6 +29,8 @@ COLUMNS = (Q_HEADS + 2 * KV_HEADS) * HEAD
 GROUPS = COLUMNS // GROUP
 Q_GROUPS = Q_HEADS // GROUP_HEADS
 QUANT = TILES * P * PACK
+GAIN_AHEAD = 2
+SCALAR_GROUPS = 2
 
 FLOPS = 2 * BATCHES * TOKENS * HIDDEN * COLUMNS
 
@@ -42,7 +44,7 @@ def tile_attentionlayerdecoder_pa_t_kernel(
         const = ctx.enter_context(tc.tile_pool(name="const", bufs=1))
         stats = ctx.enter_context(tc.tile_pool(name="stats", bufs=3))
         squares = ctx.enter_context(tc.tile_pool(name="squares", bufs=4))
-        gained = ctx.enter_context(tc.tile_pool(name="gained", bufs=3))
+        gained = ctx.enter_context(tc.tile_pool(name="gained", bufs=GAIN_AHEAD + 1))
         normed = ctx.enter_context(tc.tile_pool(name="normed", bufs=2))
         packed = ctx.enter_context(tc.tile_pool(name="packed", bufs=2))
         results = ctx.enter_context(tc.tile_pool(name="results", bufs=6))
@@ -59,18 +61,8 @@ def tile_attentionlayerdecoder_pa_t_kernel(
         nc.vector.memset(ones[:], 1.0)
         ident = const.tile([P, P], F32)
         masks.make_identity(nc, ident[:])
-
-        nc.scalar.dma_start(out=gain_row[0:1, :], in_=norm_w.unsqueeze(0))
-        q_columns = Q_HEADS * HEAD
-        kv_columns = KV_HEADS * HEAD
-        nc.scalar.dma_start(out=bias_row[0:1, 0:q_columns], in_=bq.unsqueeze(0))
-        nc.scalar.dma_start(
-            out=bias_row[0:1, q_columns : q_columns + kv_columns], in_=bk.unsqueeze(0)
-        )
-        nc.scalar.dma_start(out=bias_row[0:1, q_columns + kv_columns : COLUMNS], in_=bv.unsqueeze(0))
-
         table_warm = const.tile([P, 1], F32)
-        nc.scalar.activation(out=table_warm[:], in_=eps[:], func=ACT.Sqrt)
+        nc.scalar.activation(out=table_warm[:], in_=eps[:], func=ACT.Abs_reciprocal_sqrt)
 
         token_tiles = {}
 
@@ -90,12 +82,18 @@ def tile_attentionlayerdecoder_pa_t_kernel(
                 in_=rows.rearrange("(r p) k -> p r k", p=P),
             )
 
+        q_columns = Q_HEADS * HEAD
+        kv_columns = KV_HEADS * HEAD
         load_tokens(0)
+        nc.sync.dma_start(out=gain_row[0:1, :], in_=norm_w.unsqueeze(0))
         load_tokens(1)
         for g in range(Q_GROUPS):
             load_weight_rows(g * GROUP_HEADS, Wq[g * GROUP : (g + 1) * GROUP, :])
         load_weight_rows(Q_HEADS, Wk)
         load_weight_rows(Q_HEADS + KV_HEADS, Wv)
+        nc.sync.dma_start(out=bias_row[0:1, 0:q_columns], in_=bq.unsqueeze(0))
+        nc.sync.dma_start(out=bias_row[0:1, q_columns : q_columns + kv_columns], in_=bk.unsqueeze(0))
+        nc.sync.dma_start(out=bias_row[0:1, q_columns + kv_columns : COLUMNS], in_=bv.unsqueeze(0))
         for b in range(2, BATCHES):
             load_tokens(b)
 
@@ -105,42 +103,50 @@ def tile_attentionlayerdecoder_pa_t_kernel(
             nc.vector.tensor_copy(out=out, in_=spread[:])
 
         gain = const.tile([P, HIDDEN], BF16)
-        repeat_row(gain_row[:], gain[:])
         bias = const.tile([P, COLUMNS], F32)
-        for g in range(GROUPS):
-            repeat_row(bias_row[:, g * GROUP : (g + 1) * GROUP], bias[:, g * GROUP : (g + 1) * GROUP])
 
-        square_sum, root, inverse_root, gained_tokens = {}, {}, {}, {}
-        x_codes, x_scales = {}, {}
+        inverse_root, gained_tokens, x_codes, x_scales = {}, {}, {}, {}
 
-        def apply_gain(b):
-            gained_tokens[b] = gained.tile([P, TILES, HIDDEN], F32, name="gained_tokens")
+        def apply_gain(b, half):
+            if half == 0:
+                gained_tokens[b] = gained.tile([P, TILES, HIDDEN], F32, name="gained_tokens")
+            two = slice(2 * half, 2 * half + 2)
+            nc.gpsimd.tensor_tensor(
+                out=gained_tokens[b][:, two, :],
+                in0=token_tiles[b][:, two, :],
+                in1=gain[:].unsqueeze(1).to_broadcast([P, 2, HIDDEN]),
+                op=ALU.mult,
+            )
+
+        def take_stats(b):
+            square_sum = stats.tile([P, TILES], F32, name="square_sum")
             for j in range(TILES):
-                nc.gpsimd.tensor_tensor(
-                    out=gained_tokens[b][:, j, :], in0=token_tiles[b][:, j, :], in1=gain[:], op=ALU.mult
-                )
-
-        def sum_squares(b, tiles):
-            if b not in square_sum:
-                square_sum[b] = stats.tile([P, TILES], F32, name="square_sum")
-            for j in tiles:
                 unread = squares.tile([P, HIDDEN], BF16, name="unread")
                 nc.scalar.activation(
                     out=unread[:],
                     in_=token_tiles[b][:, j, :],
                     func=ACT.Square,
-                    accum_out=square_sum[b][:, j : j + 1],
+                    accum_out=square_sum[:, j : j + 1],
                 )
-
-        def root_mean_square(b):
-            root[b] = stats.tile([P, TILES], F32, name="root")
+            inverse_root[b] = stats.tile([P, TILES], F32, name="inverse_root")
             nc.scalar.activation(
-                out=root[b][:], in_=square_sum[b][:], func=ACT.Sqrt, bias=eps[:], scale=1.0 / HIDDEN
+                out=inverse_root[b][:],
+                in_=square_sum[:],
+                func=ACT.Abs_reciprocal_sqrt,
+                bias=eps[:],
+                scale=1.0 / HIDDEN,
             )
 
-        def invert_root(b):
-            inverse_root[b] = stats.tile([P, TILES], F32, name="inverse_root")
-            nc.vector.reciprocal(out=inverse_root[b][:], in_=root[b][:])
+        def normalise(b):
+            x = normed.tile([P, TILES * HIDDEN], BF16, name="x")
+            for j in range(TILES):
+                nc.scalar.activation(
+                    out=x[:, j * HIDDEN : (j + 1) * HIDDEN],
+                    in_=gained_tokens[b][:, j, :],
+                    func=ACT.Copy,
+                    scale=inverse_root[b][:, j : j + 1],
+                )
+            return x
 
         def k_to_partitions(row_words, grouped_words, copy):
             for pair in range(TILES // 2):
@@ -163,20 +169,12 @@ def tile_attentionlayerdecoder_pa_t_kernel(
         def as_grouped_words(tile_2d):
             return tile_2d.bitcast(F32).rearrange("p (i n u) -> p i n u", i=TILES, u=HALVES)
 
-        def normalise(b):
-            x = normed.tile([P, TILES * HIDDEN], BF16, name="x")
-            for j in range(TILES):
-                nc.scalar.activation(
-                    out=x[:, j * HIDDEN : (j + 1) * HIDDEN],
-                    in_=gained_tokens[b][:, j, :],
-                    func=ACT.Copy,
-                    scale=inverse_root[b][:, j : j + 1],
-                )
-            return x
-
-        def pack_x(b, x):
+        def flip_x(x):
             grouped = normed.tile([P, QUANT], BF16, name="grouped", align_bytes=64)
             k_to_partitions(as_row_words(x[:]), as_grouped_words(grouped[:]), nc.scalar.copy)
+            return grouped
+
+        def quantise_x(b, grouped):
             x_codes[b] = packed.tile([P, TILES * P], U32, name="x_codes", align_bytes=64)
             x_scales[b] = packed.tile([P, TILES * P], U8, name="x_scales", align_bytes=64)
             nc.vector.quantize_mx(
@@ -202,15 +200,9 @@ def tile_attentionlayerdecoder_pa_t_kernel(
         def by_head(columns):
             return columns.rearrange("p (h d) -> p h d", d=HEAD)
 
-        def store(heads_out, y_heads):
-            nc.sync.dma_start(
-                out=heads_out.rearrange("h (p j) d -> p h (j d)", j=TILES),
-                in_=y_heads.rearrange("p h j d -> p h (j d)"),
-            )
-
-        def project(b, g):
+        def multiply(b, g):
             columns = slice(g * GROUP, (g + 1) * GROUP)
-            y = results.tile([P, GROUP_HEADS, TILES, HEAD], F32, name="y")
+            banks = []
             for j in range(TILES):
                 rows = slice(j * P, (j + 1) * P)
                 acc = sums.tile([P, GROUP], F32, name="acc")
@@ -223,46 +215,65 @@ def tile_attentionlayerdecoder_pa_t_kernel(
                     start=True,
                     stop=True,
                 )
-                nc.vector.tensor_tensor(
-                    out=y[:, :, j, :], in0=by_head(acc[:]), in1=by_head(bias[:, columns]), op=ALU.add
-                )
+                banks.append(acc)
+            return banks
+
+        def store(heads_out, y_heads):
+            nc.sync.dma_start(
+                out=heads_out.rearrange("h (p j) d -> p h (j d)", j=TILES),
+                in_=y_heads.rearrange("p h j d -> p h (j d)"),
+            )
+
+        def add_bias_and_store(b, g, banks):
+            columns = slice(g * GROUP, (g + 1) * GROUP)
+            y = results.tile([P, GROUP_HEADS, TILES, HEAD], F32, name="y")
+            for j in range(TILES):
+                if j == 0 and g < SCALAR_GROUPS:
+                    nc.scalar.copy(out=y[:, :, j, :], in_=by_head(banks[j][:]))
+                    nc.gpsimd.tensor_tensor(
+                        out=y[:, :, j, :], in0=y[:, :, j, :], in1=by_head(bias[:, columns]), op=ALU.add
+                    )
+                else:
+                    nc.vector.tensor_tensor(
+                        out=y[:, :, j, :],
+                        in0=by_head(banks[j][:]),
+                        in1=by_head(bias[:, columns]),
+                        op=ALU.add,
+                    )
             if g < Q_GROUPS:
                 store(q_out[b, g * GROUP_HEADS : (g + 1) * GROUP_HEADS], y[:])
             else:
                 store(k_out[b], y[:, 0:KV_HEADS])
                 store(v_out[b], y[:, KV_HEADS : 2 * KV_HEADS])
 
-        first_half = range(0, TILES // 2)
-        second_half = range(TILES // 2, TILES)
-
-        def finish_stats(b):
-            if b < BATCHES:
-                sum_squares(b, second_half)
-                root_mean_square(b)
-            if b + 1 < BATCHES:
-                sum_squares(b + 1, first_half)
-
-        gain_ahead = 3
-        for b in range(gain_ahead):
-            apply_gain(b)
-        sum_squares(0, first_half)
-        finish_stats(0)
-        invert_root(0)
+        repeat_row(gain_row[:], gain[:])
+        for b in range(GAIN_AHEAD):
+            apply_gain(b, 0)
+            apply_gain(b, 1)
+        take_stats(0)
         for g in range(GROUPS):
             pack_weights(g)
-        pack_x(0, normalise(0))
-        finish_stats(1)
+        for g in range(GROUPS):
+            repeat_row(bias_row[:, g * GROUP : (g + 1) * GROUP], bias[:, g * GROUP : (g + 1) * GROUP])
+        quantise_x(0, flip_x(normalise(0)))
+        take_stats(1)
 
         for b in range(BATCHES):
             following = b + 1 < BATCHES
+            gain_due = b + GAIN_AHEAD < BATCHES
+            add_bias_and_store(b, 0, multiply(b, 0))
+            if gain_due:
+                apply_gain(b + GAIN_AHEAD, 0)
             if following:
-                invert_root(b + 1)
                 x_next = normalise(b + 1)
-            project(b, 0)
-            project(b, 1)
+            banks = multiply(b, 1)
             if following:
-                pack_x(b + 1, x_next)
-            finish_stats(b + 2)
-            project(b, 2)
-            if b + gain_ahead < BATCHES:
-                apply_gain(b + gain_ahead)
+                grouped_next = flip_x(x_next)
+            add_bias_and_store(b, 1, banks)
+            if gain_due:
+                apply_gain(b + GAIN_AHEAD, 1)
+            if following:
+                quantise_x(b + 1, grouped_next)
+            if b + 2 < BATCHES:
+                take_stats(b + 2)
+            add_bias_and_store(b, 2, multiply(b, 2))

@@ -30,7 +30,7 @@ GROUPS = COLUMNS // GROUP
 Q_GROUPS = Q_HEADS // GROUP_HEADS
 QUANT = TILES * P * PACK
 GAIN_AHEAD = 2
-SCALAR_GROUPS = 2
+SCALAR_GROUPS = 3
 
 FLOPS = 2 * BATCHES * TOKENS * HIDDEN * COLUMNS
 

@@ -30,7 +30,7 @@ GROUPS = COLUMNS // GROUP
 Q_GROUPS = Q_HEADS // GROUP_HEADS
 QUANT = TILES * P * PACK
 GAIN_AHEAD = 2
-SCALAR_GROUPS = 3
+SCALAR_GROUPS = 2
 
 FLOPS = 2 * BATCHES * TOKENS * HIDDEN * COLUMNS
 
@@ -53,12 +53,6 @@ def tile_attentionlayerdecoder_pa_t_kernel(
 
         eps = const.tile([P, 1], F32)
         nc.vector.memset(eps[:], EPS)
-        gain_row = const.tile([P, HIDDEN], BF16)
-        nc.vector.memset(gain_row[:], 0.0)
-        bias_row = const.tile([P, COLUMNS], BF16)
-        nc.vector.memset(bias_row[:], 0.0)
-        ones = const.tile([P, P], BF16)
-        nc.vector.memset(ones[:], 1.0)
         ident = const.tile([P, P], F32)
         masks.make_identity(nc, ident[:])
         table_warm = const.tile([P, 1], F32)
@@ -82,28 +76,24 @@ def tile_attentionlayerdecoder_pa_t_kernel(
                 in_=rows.rearrange("(r p) k -> p r k", p=P),
             )
 
+        gain = const.tile([P, HIDDEN], BF16)
+        bias = const.tile([P, COLUMNS], BF16)
         q_columns = Q_HEADS * HEAD
         kv_columns = KV_HEADS * HEAD
+        nc.sync.dma_start(out=gain[:], in_=norm_w.partition_broadcast(P))
         load_tokens(0)
-        nc.sync.dma_start(out=gain_row[0:1, :], in_=norm_w.unsqueeze(0))
-        load_tokens(1)
         for g in range(Q_GROUPS):
             load_weight_rows(g * GROUP_HEADS, Wq[g * GROUP : (g + 1) * GROUP, :])
         load_weight_rows(Q_HEADS, Wk)
         load_weight_rows(Q_HEADS + KV_HEADS, Wv)
-        nc.sync.dma_start(out=bias_row[0:1, 0:q_columns], in_=bq.unsqueeze(0))
-        nc.sync.dma_start(out=bias_row[0:1, q_columns : q_columns + kv_columns], in_=bk.unsqueeze(0))
-        nc.sync.dma_start(out=bias_row[0:1, q_columns + kv_columns : COLUMNS], in_=bv.unsqueeze(0))
+        load_tokens(1)
+        nc.sync.dma_start(out=bias[:, 0:q_columns], in_=bq.partition_broadcast(P))
+        nc.sync.dma_start(
+            out=bias[:, q_columns : q_columns + kv_columns], in_=bk.partition_broadcast(P)
+        )
+        nc.sync.dma_start(out=bias[:, q_columns + kv_columns : COLUMNS], in_=bv.partition_broadcast(P))
         for b in range(2, BATCHES):
             load_tokens(b)
-
-        def repeat_row(row, out):
-            spread = sums.tile([P, GROUP], F32, name="acc")
-            nc.tensor.matmul(out=spread[:], lhsT=ones[:], rhs=row, start=True, stop=True)
-            nc.vector.tensor_copy(out=out, in_=spread[:])
-
-        gain = const.tile([P, HIDDEN], BF16)
-        bias = const.tile([P, COLUMNS], F32)
 
         inverse_root, gained_tokens, x_codes, x_scales = {}, {}, {}, {}
 
@@ -225,10 +215,11 @@ def tile_attentionlayerdecoder_pa_t_kernel(
             )
 
         def add_bias_and_store(b, g, banks):
+            scalar_tiles = 1 if b + GAIN_AHEAD < BATCHES else 2
             columns = slice(g * GROUP, (g + 1) * GROUP)
             y = results.tile([P, GROUP_HEADS, TILES, HEAD], F32, name="y")
             for j in range(TILES):
-                if j == 0 and g < SCALAR_GROUPS:
+                if j < scalar_tiles and g < SCALAR_GROUPS:
                     nc.scalar.copy(out=y[:, :, j, :], in_=by_head(banks[j][:]))
                     nc.gpsimd.tensor_tensor(
                         out=y[:, :, j, :], in0=y[:, :, j, :], in1=by_head(bias[:, columns]), op=ALU.add
@@ -246,15 +237,12 @@ def tile_attentionlayerdecoder_pa_t_kernel(
                 store(k_out[b], y[:, 0:KV_HEADS])
                 store(v_out[b], y[:, KV_HEADS : 2 * KV_HEADS])
 
-        repeat_row(gain_row[:], gain[:])
         for b in range(GAIN_AHEAD):
             apply_gain(b, 0)
             apply_gain(b, 1)
         take_stats(0)
         for g in range(GROUPS):
             pack_weights(g)
-        for g in range(GROUPS):
-            repeat_row(bias_row[:, g * GROUP : (g + 1) * GROUP], bias[:, g * GROUP : (g + 1) * GROUP])
         quantise_x(0, flip_x(normalise(0)))
         take_stats(1)
 

from contextlib import ExitStack

import concourse.masks as masks
import concourse.mybir as mybir

F32 = mybir.dt.float32
BF16 = mybir.dt.bfloat16
U32 = mybir.dt.uint32
U8 = mybir.dt.uint8
FP8X4 = mybir.dt.float8_e4m3fn_x4
ACT = mybir.ActivationFunctionType
ALU = mybir.AluOpType

P = 128
BATCHES = 8
TOKENS = 512
HIDDEN = 512
HEAD = 128
Q_HEADS = 8
KV_HEADS = 2
EPS = 2.0**-23

TILES = TOKENS // P
PACK = 4
HALVES = 2
GROUP_HEADS = 4
GROUP = GROUP_HEADS * HEAD
COLUMNS = (Q_HEADS + 2 * KV_HEADS) * HEAD
GROUPS = COLUMNS // GROUP
Q_GROUPS = Q_HEADS // GROUP_HEADS
QUANT = TILES * P * PACK
GAIN_AHEAD = 2
SCALAR_GROUPS = 2

FLOPS = 2 * BATCHES * TOKENS * HIDDEN * COLUMNS


def tile_attentionlayerdecoder_pa_t_kernel(
    tc, tokens, norm_w, Wq, bq, Wk, bk, Wv, bv, q_out, k_out, v_out
):
    nc = tc.nc
    with ExitStack() as ctx:
        ctx.enter_context(tc.manual_schedule())
        const = ctx.enter_context(tc.tile_pool(name="const", bufs=1))
        stats = ctx.enter_context(tc.tile_pool(name="stats", bufs=3))
        squares = ctx.enter_context(tc.tile_pool(name="squares", bufs=4))
        gained = ctx.enter_context(tc.tile_pool(name="gained", bufs=GAIN_AHEAD + 1))
        normed = ctx.enter_context(tc.tile_pool(name="normed", bufs=2))
        packed = ctx.enter_context(tc.tile_pool(name="packed", bufs=2))
        results = ctx.enter_context(tc.tile_pool(name="results", bufs=6))
        flipped = ctx.enter_context(tc.psum_pool(name="flipped", bufs=3))
        sums = ctx.enter_context(tc.psum_pool(name="sums", bufs=5))

        eps = const.tile([P, 1], F32)
        nc.vector.memset(eps[:], EPS)
        ident = const.tile([P, P], F32)
        masks.make_identity(nc, ident[:])
        table_warm = const.tile([P, 1], F32)
        nc.scalar.activation(out=table_warm[:], in_=eps[:], func=ACT.Abs_reciprocal_sqrt)

        token_tiles = {}

        def load_tokens(b):
            token_tiles[b] = const.tile([P, TILES, HIDDEN], BF16, name="tokens%d" % b)
            nc.sync.dma_start(
                out=token_tiles[b][:], in_=tokens[b].rearrange("(p j) k -> p j k", j=TILES)
            )

        w_raw = const.tile([P, COLUMNS // P * HIDDEN], BF16)
        w_rows = w_raw[:].rearrange("p (r k) -> p r k", k=HIDDEN)

        def load_weight_rows(first_tile, rows):
            n_tiles = rows.shape[0] // P
            nc.sync.dma_start(
                out=w_rows[:, first_tile : first_tile + n_tiles, :],
                in_=rows.rearrange("(r p) k -> p r k", p=P),
            )

        gain = const.tile([P, HIDDEN], BF16)
        bias = const.tile([P, COLUMNS], BF16)
        q_columns = Q_HEADS * HEAD
        kv_columns = KV_HEADS * HEAD
        nc.sync.dma_start(out=gain[:], in_=norm_w.partition_broadcast(P))
        load_tokens(0)
        for g in range(Q_GROUPS):
            load_weight_rows(g * GROUP_HEADS, Wq[g * GROUP : (g + 1) * GROUP, :])
        load_weight_rows(Q_HEADS, Wk)
        load_weight_rows(Q_HEADS + KV_HEADS, Wv)
        load_tokens(1)
        nc.sync.dma_start(out=bias[:, 0:q_columns], in_=bq.partition_broadcast(P))
        nc.sync.dma_start(
            out=bias[:, q_columns : q_columns + kv_columns], in_=bk.partition_broadcast(P)
        )
        nc.sync.dma_start(out=bias[:, q_columns + kv_columns : COLUMNS], in_=bv.partition_broadcast(P))
        for b in range(2, BATCHES):
            load_tokens(b)

        inverse_root, gained_tokens, x_codes, x_scales = {}, {}, {}, {}

        def apply_gain(b, half):
            if half == 0:
                gained_tokens[b] = gained.tile([P, TILES, HIDDEN], F32, name="gained_tokens")
            two = slice(2 * half, 2 * half + 2)
            nc.gpsimd.tensor_tensor(
                out=gained_tokens[b][:, two, :],
                in0=token_tiles[b][:, two, :],
                in1=gain[:].unsqueeze(1).to_broadcast([P, 2, HIDDEN]),
                op=ALU.mult,
            )

        def take_stats(b):
            square_sum = stats.tile([P, TILES], F32, name="square_sum")
            for j in range(TILES):
                unread = squares.tile([P, HIDDEN], BF16, name="unread")
                nc.scalar.activation(
                    out=unread[:],
                    in_=token_tiles[b][:, j, :],
                    func=ACT.Square,
                    accum_out=square_sum[:, j : j + 1],
                )
            inverse_root[b] = stats.tile([P, TILES], F32, name="inverse_root")
            nc.scalar.activation(
                out=inverse_root[b][:],
                in_=square_sum[:],
                func=ACT.Abs_reciprocal_sqrt,
                bias=eps[:],
                scale=1.0 / HIDDEN,
            )

        def normalise(b):
            x = normed.tile([P, TILES * HIDDEN], BF16, name="x")
            for j in range(TILES):
                nc.scalar.activation(
                    out=x[:, j * HIDDEN : (j + 1) * HIDDEN],
                    in_=gained_tokens[b][:, j, :],
                    func=ACT.Copy,
                    scale=inverse_root[b][:, j : j + 1],
                )
            return x

        def k_to_partitions(row_words, grouped_words, copy):
            for pair in range(TILES // 2):
                flip = flipped.tile([P, 2, HALVES, P], F32, name="flip")
                for i in range(2):
                    for u in range(HALVES):
                        nc.tensor.transpose(
                            out=flip[:, i, u, :],
                            in_=row_words[:, 2 * pair + i, u * P : (u + 1) * P],
                            identity=ident[:],
                        )
                copy(
                    out=grouped_words[:, 2 * pair : 2 * pair + 2, :, :],
                    in_=flip[:].rearrange("p i u n -> p i n u"),
                )

        def as_row_words(tile_2d):
            return tile_2d.bitcast(F32).rearrange("p (i w) -> p i w", i=TILES)

        def as_grouped_words(tile_2d):
            return tile_2d.bitcast(F32).rearrange("p (i n u) -> p i n u", i=TILES, u=HALVES)

        def flip_x(x):
            grouped = normed.tile([P, QUANT], BF16, name="grouped", align_bytes=64)
            k_to_partitions(as_row_words(x[:]), as_grouped_words(grouped[:]), nc.scalar.copy)
            return grouped

        def quantise_x(b, grouped):
            x_codes[b] = packed.tile([P, TILES * P], U32, name="x_codes", align_bytes=64)
            x_scales[b] = packed.tile([P, TILES * P], U8, name="x_scales", align_bytes=64)
            nc.vector.quantize_mx(
                out=x_codes[b][:].bitcast(FP8X4), scales=x_scales[b][:], in_=grouped[:]
            )

        w_grouped = const.tile([P, GROUPS * QUANT], BF16, align_bytes=64)
        w_codes = const.tile([P, COLUMNS], U32, align_bytes=64)
        w_scales = const.tile([P, COLUMNS], U8, align_bytes=64)

        def pack_weights(g):
            k_to_partitions(
                as_row_words(w_raw[:, g * GROUP_HEADS * HIDDEN : (g + 1) * GROUP_HEADS * HIDDEN]),
                as_grouped_words(w_grouped[:, g * QUANT : (g + 1) * QUANT]),
                nc.vector.tensor_copy,
            )
            nc.vector.quantize_mx(
                out=w_codes[:, g * GROUP : (g + 1) * GROUP].bitcast(FP8X4),
                scales=w_scales[:, g * GROUP : (g + 1) * GROUP],
                in_=w_grouped[:, g * QUANT : (g + 1) * QUANT],
            )

        def by_head(columns):
            return columns.rearrange("p (h d) -> p h d", d=HEAD)

        def multiply(b, g):
            columns = slice(g * GROUP, (g + 1) * GROUP)
            banks = []
            for j in range(TILES):
                rows = slice(j * P, (j + 1) * P)
                acc = sums.tile([P, GROUP], F32, name="acc")
                nc.tensor.matmul_mx(
                    out=acc[:],
                    lhsT=x_codes[b][:, rows].bitcast(FP8X4),
                    lhsT_scale=x_scales[b][:, rows],
                    rhs=w_codes[:, columns].bitcast(FP8X4),
                    rhs_scale=w_scales[:, columns],
                    start=True,
                    stop=True,
                )
                banks.append(acc)
            return banks

        def store(heads_out, y_heads):
            nc.sync.dma_start(
                out=heads_out.rearrange("h (p j) d -> p h (j d)", j=TILES),
                in_=y_heads.rearrange("p h j d -> p h (j d)"),
            )

        def add_bias_and_store(b, g, banks):
            scalar_tiles = 1 if b + GAIN_AHEAD < BATCHES else 2
            columns = slice(g * GROUP, (g + 1) * GROUP)
            y = results.tile([P, GROUP_HEADS, TILES, HEAD], F32, name="y")
            for j in range(TILES):
                if j < scalar_tiles and g < SCALAR_GROUPS:
                    nc.scalar.copy(out=y[:, :, j, :], in_=by_head(banks[j][:]))
                    nc.gpsimd.tensor_tensor(
                        out=y[:, :, j, :], in0=y[:, :, j, :], in1=by_head(bias[:, columns]), op=ALU.add
                    )
                else:
                    nc.vector.tensor_tensor(
                        out=y[:, :, j, :],
                        in0=by_head(banks[j][:]),
                        in1=by_head(bias[:, columns]),
                        op=ALU.add,
                    )
            if g < Q_GROUPS:
                store(q_out[b, g * GROUP_HEADS : (g + 1) * GROUP_HEADS], y[:])
            else:
                store(k_out[b], y[:, 0:KV_HEADS])
                store(v_out[b], y[:, KV_HEADS : 2 * KV_HEADS])

        for b in range(GAIN_AHEAD):
            apply_gain(b, 0)
            apply_gain(b, 1)
        take_stats(0)
        for g in range(GROUPS):
            pack_weights(g)
        quantise_x(0, flip_x(normalise(0)))
        take_stats(1)

        for b in range(BATCHES):
            following = b + 1 < BATCHES
            gain_due = b + GAIN_AHEAD < BATCHES
            add_bias_and_store(b, 0, multiply(b, 0))
            if gain_due:
                apply_gain(b + GAIN_AHEAD, 0)
            if following:
                x_next = normalise(b + 1)
            banks = multiply(b, 1)
            if following:
                grouped_next = flip_x(x_next)
            add_bias_and_store(b, 1, banks)
            if gain_due:
                apply_gain(b + GAIN_AHEAD, 1)
            if following:
                quantise_x(b + 1, grouped_next)
            if b + 2 < BATCHES:
                take_stats(b + 2)
            add_bias_and_store(b, 2, multiply(b, 2))
